import numpy as np
import ml_dtypes


def mxq(x, axis, fmt="e4m3"):
    dtype, down = {"e4m3": (ml_dtypes.float8_e4m3fn, 7), "e5m2": (ml_dtypes.float8_e5m2, 14)}[fmt]
    v = np.moveaxis(np.asarray(x, np.float32).astype(ml_dtypes.bfloat16).astype(np.float64), axis, -1)
    blocks = v.reshape(v.shape[:-1] + (-1, 32))
    amax = np.abs(blocks).max(-1, keepdims=True)
    byte = np.maximum(np.where(amax > 0, np.frexp(amax)[1] - 1 + 127, 0) - down, 1)
    scale = np.exp2(byte - 127.0)
    codes = (blocks / scale).astype(np.float32).astype(dtype).astype(np.float64)
    return np.moveaxis((codes * scale).reshape(v.shape), -1, axis)


WIDE = False


def mx_kscale(k):
    if not WIDE:
        return np.ones(k)
    levels = np.array([10, -10, 5, -5, 0])
    a = np.random.permutation(np.resize(levels, k // 512 * 4)).reshape(k // 512, 4)
    idx = np.arange(k)
    return np.exp2(a[idx // 512, idx % 128 // 32])


BF16 = ml_dtypes.bfloat16


def bf(x):
    return np.asarray(x, np.float32).astype(BF16)


def f64(x):
    return np.asarray(x).astype(np.float64)


E2M1 = np.array([0.0, 0.5, 1.0, 1.5, 2.0, 3.0, 4.0, 6.0, -0.0, -0.5, -1.0, -1.5, -2.0, -3.0, -4.0, -6.0])


def pack_weight(w, fmt):
    k, n = w.shape
    w = f64(bf(w)).reshape(k // 32, 32, n)
    amax = np.abs(w).max(1)
    if fmt == "e4m3":
        byte = np.frexp(amax)[1] - 1 + 127 - 7
    else:
        mant, ex = np.frexp(amax / 6.0)
        byte = np.where(mant > 0.5, ex, ex - 1) + 127
    byte = np.clip(np.where(amax > 0, byte, 1), 1, 254)
    scaled = (w * np.exp2(127.0 - byte)[:, None, :]).reshape(k, n).astype(np.float32)
    by_word = np.ascontiguousarray(scaled.reshape(k // 512, 128, 4, n).transpose(0, 1, 3, 2))
    if fmt == "e4m3":
        words = by_word.astype(ml_dtypes.float8_e4m3fn).view(np.uint8)
    else:
        c = by_word.astype(ml_dtypes.float4_e2m1fn).view(np.uint8) & 0xF
        words = c[..., 0::2] | (c[..., 1::2] << 4)
    return np.ascontiguousarray(words), np.ascontiguousarray(byte.astype(np.uint8).reshape(k // 512, 16, n))


def unpack_weight(words, scales, fmt):
    g, p, n, _ = words.shape
    if fmt == "e4m3":
        vals = np.ascontiguousarray(words).view(ml_dtypes.float8_e4m3fn).astype(np.float64)
    else:
        nib = np.empty((g, p, n, 4), np.uint8)
        nib[..., 0::2] = words & 0xF
        nib[..., 1::2] = words >> 4
        vals = E2M1[nib]
    vals = vals * np.repeat(np.exp2(scales.astype(np.float64) - 127.0), 8, axis=1)[..., None]
    return vals.transpose(0, 1, 3, 2).reshape(g * 512, n)


BATCH, IN_LEN, HID_LEN = 128, 1024, 2048
FMT = "e4m3"


def sigmoid(v):
    return 1.0 / (1.0 + np.exp(-v))


def setup_inputs():
    s, t = mx_kscale(IN_LEN), mx_kscale(HID_LEN)
    d = {
        "x": bf(np.random.standard_normal((BATCH, IN_LEN)) * s),
        "h": bf(np.random.standard_normal((BATCH, HID_LEN)) * t),
        "c_prev": bf(np.random.standard_normal((BATCH, HID_LEN))),
    }
    for g in range(4):
        w = np.random.standard_normal((HID_LEN, IN_LEN)) * 0.7 / np.sqrt(IN_LEN) / s
        d[f"w{g+1}_words"], d[f"w{g+1}_scales"] = pack_weight(np.ascontiguousarray(w.T), FMT)
        d[f"b{g+1}"] = bf(np.random.standard_normal(HID_LEN) * 0.5)
        r = np.random.standard_normal((HID_LEN, HID_LEN)) * 0.7 / np.sqrt(HID_LEN) / t
        d[f"r{g+1}_words"], d[f"r{g+1}_scales"] = pack_weight(np.ascontiguousarray(r.T), FMT)
    return d


def reference(x, h, c_prev, w1_words, w1_scales, b1, r1_words, r1_scales, w2_words, w2_scales, b2, r2_words, r2_scales, w3_words, w3_scales, b3, r3_words, r3_scales, w4_words, w4_scales, b4, r4_words, r4_scales):
    W = np.concatenate([unpack_weight(w1_words, w1_scales, FMT).T, unpack_weight(w2_words, w2_scales, FMT).T, unpack_weight(w3_words, w3_scales, FMT).T, unpack_weight(w4_words, w4_scales, FMT).T], axis=0)
    R = np.concatenate([unpack_weight(r1_words, r1_scales, FMT).T, unpack_weight(r2_words, r2_scales, FMT).T, unpack_weight(r3_words, r3_scales, FMT).T, unpack_weight(r4_words, r4_scales, FMT).T], axis=0)
    B = np.concatenate([f64(b1), f64(b2), f64(b3), f64(b4)], axis=0)
    gates = (mxq(f64(x), 1, "e4m3") @ W.T) + (mxq(f64(h), 1, "e4m3") @ R.T) + B
    gf, gi, gc, go = np.split(gates, 4, axis=-1)
    f = sigmoid(gf)
    i = sigmoid(gi)
    g = np.tanh(gc)
    o = sigmoid(go)
    c_next = f * f64(c_prev) + i * g
    h_next = o * np.tanh(c_next)
    return (h_next, c_next)

@@ -1,0 +1,214 @@
+import concourse.mybir as mybir
+from concourse.masks import make_identity
+
+F32 = mybir.dt.float32
+BF16 = mybir.dt.bfloat16
+I32 = mybir.dt.int32
+U32 = mybir.dt.uint32
+U8 = mybir.dt.uint8
+FP8X4 = mybir.dt.float8_e4m3fn_x4
+ACT = mybir.ActivationFunctionType
+ADD = mybir.AluOpType.add
+
+P = 128
+PACK = 4
+K_PASS = P * PACK
+IN_LEN = 1024
+HID = 2048
+X_PASSES = IN_LEN // K_PASS
+H_PASSES = HID // K_PASS
+PASSES = X_PASSES + H_PASSES
+GATES = 4
+N_TILE = 512
+BLOCKS = HID // N_TILE
+QUADRANTS = 4
+WORDS_PER_PASS = K_PASS // 2
+
+SMALL_PER_BIG = 2
+WORD_BUFS = 12
+
+FLOPS = 2 * P * (IN_LEN + HID) * GATES * HID
+
+
+def tile_my_lstm_cell_w_kernel(
+    tc,
+    x,
+    h,
+    c_prev,
+    w1_words,
+    w1_scales,
+    b1,
+    r1_words,
+    r1_scales,
+    w2_words,
+    w2_scales,
+    b2,
+    r2_words,
+    r2_scales,
+    w3_words,
+    w3_scales,
+    b3,
+    r3_words,
+    r3_scales,
+    w4_words,
+    w4_scales,
+    b4,
+    r4_words,
+    r4_scales,
+    out_0,
+    out_1,
+):
+    nc = tc.nc
+    gate_inputs = [
+        (w1_words, w1_scales, b1, r1_words, r1_scales),
+        (w2_words, w2_scales, b2, r2_words, r2_scales),
+        (w3_words, w3_scales, b3, r3_words, r3_scales),
+        (w4_words, w4_scales, b4, r4_words, r4_scales),
+    ]
+
+    with (
+        tc.manual_schedule(),
+        tc.tile_pool(name="keep", bufs=1) as keep,
+        tc.tile_pool(name="stream", bufs=WORD_BUFS) as stream,
+        tc.tile_pool(name="bias", bufs=2) as bias_pool,
+        tc.tile_pool(name="sums", bufs=BLOCKS) as sums_pool,
+        tc.psum_pool(name="acc", bufs=6) as psum_acc,
+        tc.psum_pool(name="setup", bufs=2) as psum_setup,
+    ):
+        ident_f32 = keep.tile([P, P], F32)
+        make_identity(nc, ident_f32[:])
+        ident_bf16 = keep.tile([P, P], BF16)
+        make_identity(nc, ident_bf16[:])
+
+        bias_rows = keep.tile([P, N_TILE], BF16)
+        nc.vector.memset(bias_rows[:], 0.0)
+
+        planes = [keep.tile([P, 2, HID], U8, name="planes%d" % g, align_bytes=64) for g in range(GATES)]
+        for g in range(GATES):
+            nc.vector.memset(planes[g][:].bitcast(I32), 0)
+
+        small_loads = []
+        for g, (w_words, w_scales, b, r_words, r_scales) in enumerate(gate_inputs):
+            small_loads.append((bias_rows[BLOCKS * g : BLOCKS * (g + 1), :], b.rearrange("(j n) -> j n", n=N_TILE)))
+            for operand, scales in enumerate((w_scales, r_scales)):
+                rows = 4 * scales.shape[0]
+                for q in range(QUADRANTS):
+                    small_loads.append(
+                        (
+                            planes[g][32 * q : 32 * q + rows, operand, :].bitcast(I32),
+                            scales[:, 4 * q : 4 * q + 4, :].bitcast(I32),
+                        )
+                    )
+
+        def load_big(number, out, in_):
+            nc.sync.dma_start(out=out, in_=in_)
+            for small_out, small_in in small_loads[SMALL_PER_BIG * number : SMALL_PER_BIG * (number + 1)]:
+                nc.sync.dma_start(out=small_out, in_=small_in)
+
+        xh = keep.tile([P, IN_LEN + HID], BF16)
+        c_prev_sb = keep.tile([P, HID], BF16)
+        load_big(0, xh[:, :IN_LEN], x)
+        load_big(1, xh[:, IN_LEN:], h)
+        load_big(2, c_prev_sb[:], c_prev)
+        FIRST_WEIGHT_LOAD = 3
+
+        xh_words = xh[:].bitcast(F32)
+        grouped = keep.tile([P, PASSES * P * PACK], BF16, align_bytes=64)
+        act_codes = keep.tile([P, PASSES * P], U32, align_bytes=64)
+        act_scales = keep.tile([P, PASSES * P], U8, align_bytes=64)
+        for pair in range(PASSES // 2):
+            turned = psum_setup.tile([P, 2, 2, P], F32, tag="setup")
+            for s in range(2):
+                first = WORDS_PER_PASS * (2 * pair + s)
+                for u in range(2):
+                    nc.tensor.transpose(
+                        turned[:, s, u, :], xh_words[:, first + u : first + WORDS_PER_PASS : 2], ident_f32[:]
+                    )
+            values = slice(2 * P * PACK * pair, 2 * P * PACK * (pair + 1))
+            columns = slice(2 * P * pair, 2 * P * (pair + 1))
+            nc.vector.tensor_copy(
+                out=grouped[:, values].bitcast(F32).rearrange("p (s m u) -> p s m u", s=2, u=2),
+                in_=turned[:].rearrange("p s u m -> p s m u"),
+            )
+            nc.vector.quantize_mx(
+                out=act_codes[:, columns].bitcast(FP8X4), scales=act_scales[:, columns], in_=grouped[:, values]
+            )
+
+        def broadcast_bias(g):
+            bias = bias_pool.tile([P, HID], BF16)
+            for half in range(2):
+                spread = psum_setup.tile([P, 2 * N_TILE], BF16, tag="setup")
+                for s in range(2):
+                    row = BLOCKS * g + 2 * half + s
+                    nc.tensor.matmul(
+                        out=spread[:, N_TILE * s : N_TILE * (s + 1)],
+                        lhsT=ident_bf16[:, row : row + 1].to_broadcast([P, P]),
+                        rhs=bias_rows[:],
+                        start=True,
+                        stop=True,
+                    )
+                nc.scalar.copy(out=bias[:, 2 * N_TILE * half : 2 * N_TILE * (half + 1)], in_=spread[:])
+            return bias
+
+        def gate_sums(g):
+            w_words, w_scales, b, r_words, r_scales = gate_inputs[g]
+            acc = [psum_acc.tile([P, N_TILE], F32, name="acc%d" % j, tag="acc") for j in range(BLOCKS)]
+            for c in range(PASSES):
+                operand = 0 if c < X_PASSES else 1
+                group = c if c < X_PASSES else c - X_PASSES
+                words = stream.tile([P, HID], U32, align_bytes=64)
+                load_big(
+                    FIRST_WEIGHT_LOAD + PASSES * g + c,
+                    words[:].bitcast(I32),
+                    (w_words, r_words)[operand][group].rearrange("p n t -> p (n t)").bitcast(I32),
+                )
+                for j in range(BLOCKS):
+                    cols = slice(N_TILE * j, N_TILE * (j + 1))
+                    nc.tensor.matmul_mx(
+                        out=acc[j][:],
+                        lhsT=act_codes[:, P * c : P * (c + 1)].bitcast(FP8X4),
+                        lhsT_scale=act_scales[:, P * c : P * (c + 1)],
+                        rhs=words[:, cols].bitcast(FP8X4),
+                        rhs_scale=planes[g][4 * group : P, operand, cols],
+                        start=(c == 0),
+                        stop=(c == PASSES - 1),
+                    )
+            return acc
+
+        def activate(acc, bias, func, gate):
+            for j in range(BLOCKS):
+                cols = slice(N_TILE * j, N_TILE * (j + 1))
+                sums = sums_pool.tile([P, N_TILE], F32)
+                nc.vector.tensor_tensor(out=sums[:], in0=acc[j][:], in1=bias[:, cols], op=ADD)
+                nc.scalar.activation(out=gate[:, cols], in_=sums[:], func=func)
+
+        f_gate = keep.tile([P, HID], F32)
+        i_gate = keep.tile([P, HID], F32)
+        g_gate = keep.tile([P, HID], F32)
+        o_gate = keep.tile([P, HID], F32)
+        fresh = keep.tile([P, HID], F32)
+        c_next = keep.tile([P, HID], F32)
+        tanh_c = keep.tile([P, HID], F32)
+        h_next = keep.tile([P, HID], F32)
+
+        bias = broadcast_bias(0)
+        activate(gate_sums(0), bias, ACT.Sigmoid, f_gate)
+        nc.vector.tensor_mul(out=c_next[:], in0=f_gate[:], in1=c_prev_sb[:])
+
+        bias = broadcast_bias(1)
+        activate(gate_sums(1), bias, ACT.Sigmoid, i_gate)
+
+        bias = broadcast_bias(2)
+        activate(gate_sums(2), bias, ACT.Tanh, g_gate)
+        nc.vector.tensor_mul(out=fresh[:], in0=i_gate[:], in1=g_gate[:])
+        nc.vector.tensor_add(out=c_next[:], in0=c_next[:], in1=fresh[:])
+        nc.scalar.activation(out=tanh_c[:], in_=c_next[:], func=ACT.Tanh)
+
+        bias = broadcast_bias(3)
+        acc = gate_sums(3)
+        nc.sync.dma_start(out=out_1, in_=c_next[:])
+        activate(acc, bias, ACT.Sigmoid, o_gate)
+        for j in range(BLOCKS):
+            cols = slice(N_TILE * j, N_TILE * (j + 1))
+            nc.vector.tensor_mul(out=h_next[:, cols], in0=o_gate[:, cols], in1=tanh_c[:, cols])
+            nc.sync.dma_start(out=out_0[:, cols], in_=h_next[:, cols])

@@ -24,7 +24,6 @@ BLOCKS = HID // N_TILE
 QUADRANTS = 4
 WORDS_PER_PASS = K_PASS // 2
 
-SMALL_PER_BIG = 2
 WORD_BUFS = 12
 
 FLOPS = 2 * P * (IN_LEN + HID) * GATES * HID
@@ -87,30 +86,23 @@ def tile_my_lstm_cell_w_kernel(
         for g in range(GATES):
             nc.vector.memset(planes[g][:].bitcast(I32), 0)
 
-        small_loads = []
         for g, (w_words, w_scales, b, r_words, r_scales) in enumerate(gate_inputs):
-            small_loads.append((bias_rows[BLOCKS * g : BLOCKS * (g + 1), :], b.rearrange("(j n) -> j n", n=N_TILE)))
+            nc.gpsimd.dma_start(
+                out=bias_rows[BLOCKS * g : BLOCKS * (g + 1), :], in_=b.rearrange("(j n) -> j n", n=N_TILE)
+            )
             for operand, scales in enumerate((w_scales, r_scales)):
                 rows = 4 * scales.shape[0]
                 for q in range(QUADRANTS):
-                    small_loads.append(
-                        (
-                            planes[g][32 * q : 32 * q + rows, operand, :].bitcast(I32),
-                            scales[:, 4 * q : 4 * q + 4, :].bitcast(I32),
-                        )
+                    nc.gpsimd.dma_start(
+                        out=planes[g][32 * q : 32 * q + rows, operand, :].bitcast(F32),
+                        in_=scales[:, 4 * q : 4 * q + 4, :].bitcast(F32),
                     )
-
-        def load_big(number, out, in_):
-            nc.sync.dma_start(out=out, in_=in_)
-            for small_out, small_in in small_loads[SMALL_PER_BIG * number : SMALL_PER_BIG * (number + 1)]:
-                nc.sync.dma_start(out=small_out, in_=small_in)
 
         xh = keep.tile([P, IN_LEN + HID], BF16)
         c_prev_sb = keep.tile([P, HID], BF16)
-        load_big(0, xh[:, :IN_LEN], x)
-        load_big(1, xh[:, IN_LEN:], h)
-        load_big(2, c_prev_sb[:], c_prev)
-        FIRST_WEIGHT_LOAD = 3
+        nc.sync.dma_start(out=xh[:, :IN_LEN], in_=x)
+        nc.sync.dma_start(out=xh[:, IN_LEN:], in_=h)
+        nc.sync.dma_start(out=c_prev_sb[:], in_=c_prev)
 
         xh_words = xh[:].bitcast(F32)
         grouped = keep.tile([P, PASSES * P * PACK], BF16, align_bytes=64)
@@ -157,10 +149,9 @@ def tile_my_lstm_cell_w_kernel(
                 operand = 0 if c < X_PASSES else 1
                 group = c if c < X_PASSES else c - X_PASSES
                 words = stream.tile([P, HID], U32, align_bytes=64)
-                load_big(
-                    FIRST_WEIGHT_LOAD + PASSES * g + c,
-                    words[:].bitcast(I32),
-                    (w_words, r_words)[operand][group].rearrange("p n t -> p (n t)").bitcast(I32),
+                nc.sync.dma_start(
+                    out=words[:].bitcast(I32),
+                    in_=(w_words, r_words)[operand][group].rearrange("p n t -> p (n t)").bitcast(I32),
                 )
                 for j in range(BLOCKS):
                     cols = slice(N_TILE * j, N_TILE * (j + 1))

@@ -90,6 +90,7 @@ def tile_my_lstm_cell_w_kernel(
             nc.gpsimd.dma_start(
                 out=bias_rows[BLOCKS * g : BLOCKS * (g + 1), :], in_=b.rearrange("(j n) -> j n", n=N_TILE)
             )
+        for g, (w_words, w_scales, b, r_words, r_scales) in enumerate(gate_inputs):
             for operand, scales in enumerate((w_scales, r_scales)):
                 rows = 4 * scales.shape[0]
                 for q in range(QUADRANTS):

@@ -143,36 +143,38 @@ def tile_my_lstm_cell_w_kernel(
                 nc.scalar.copy(out=bias[:, 2 * N_TILE * half : 2 * N_TILE * (half + 1)], in_=spread[:])
             return bias
 
-        def gate_sums(g):
+        def block_columns(j):
+            return slice(N_TILE * j, N_TILE * (j + 1))
+
+        def gate_sums(g, blocks):
             w_words, w_scales, b, r_words, r_scales = gate_inputs[g]
-            acc = [psum_acc.tile([P, N_TILE], F32, name="acc%d" % j, tag="acc") for j in range(BLOCKS)]
+            loaded = slice(N_TILE * blocks[0], N_TILE * (blocks[-1] + 1))
+            acc = [psum_acc.tile([P, N_TILE], F32, name="acc%d" % j, tag="acc") for j in blocks]
             for c in range(PASSES):
                 operand = 0 if c < X_PASSES else 1
                 group = c if c < X_PASSES else c - X_PASSES
-                words = stream.tile([P, HID], U32, align_bytes=64)
+                words = stream.tile([P, N_TILE * len(blocks)], U32, tag="words", align_bytes=64)
                 nc.sync.dma_start(
                     out=words[:].bitcast(I32),
-                    in_=(w_words, r_words)[operand][group].rearrange("p n t -> p (n t)").bitcast(I32),
+                    in_=(w_words, r_words)[operand][group][:, loaded, :].rearrange("p n t -> p (n t)").bitcast(I32),
                 )
-                for j in range(BLOCKS):
-                    cols = slice(N_TILE * j, N_TILE * (j + 1))
+                for place, j in enumerate(blocks):
                     nc.tensor.matmul_mx(
-                        out=acc[j][:],
+                        out=acc[place][:],
                         lhsT=act_codes[:, P * c : P * (c + 1)].bitcast(FP8X4),
                         lhsT_scale=act_scales[:, P * c : P * (c + 1)],
-                        rhs=words[:, cols].bitcast(FP8X4),
-                        rhs_scale=planes[g][4 * group : P, operand, cols],
+                        rhs=words[:, block_columns(place)].bitcast(FP8X4),
+                        rhs_scale=planes[g][4 * group : P, operand, block_columns(j)],
                         start=(c == 0),
                         stop=(c == PASSES - 1),
                     )
             return acc
 
-        def activate(acc, bias, func, gate):
-            for j in range(BLOCKS):
-                cols = slice(N_TILE * j, N_TILE * (j + 1))
+        def activate(acc, blocks, bias, func, gate):
+            for place, j in enumerate(blocks):
                 sums = sums_pool.tile([P, N_TILE], F32)
-                nc.vector.tensor_tensor(out=sums[:], in0=acc[j][:], in1=bias[:, cols], op=ADD)
-                nc.scalar.activation(out=gate[:, cols], in_=sums[:], func=func)
+                nc.vector.tensor_tensor(out=sums[:], in0=acc[place][:], in1=bias[:, block_columns(j)], op=ADD)
+                nc.scalar.activation(out=gate[:, block_columns(j)], in_=sums[:], func=func)
 
         f_gate = keep.tile([P, HID], F32)
         i_gate = keep.tile([P, HID], F32)
@@ -183,24 +185,27 @@ def tile_my_lstm_cell_w_kernel(
         tanh_c = keep.tile([P, HID], F32)
         h_next = keep.tile([P, HID], F32)
 
+        all_blocks = range(BLOCKS)
         bias = broadcast_bias(0)
-        activate(gate_sums(0), bias, ACT.Sigmoid, f_gate)
+        activate(gate_sums(0, all_blocks), all_blocks, bias, ACT.Sigmoid, f_gate)
         nc.vector.tensor_mul(out=c_next[:], in0=f_gate[:], in1=c_prev_sb[:])
 
         bias = broadcast_bias(1)
-        activate(gate_sums(1), bias, ACT.Sigmoid, i_gate)
+        activate(gate_sums(1, all_blocks), all_blocks, bias, ACT.Sigmoid, i_gate)
 
         bias = broadcast_bias(2)
-        activate(gate_sums(2), bias, ACT.Tanh, g_gate)
+        activate(gate_sums(2, all_blocks), all_blocks, bias, ACT.Tanh, g_gate)
         nc.vector.tensor_mul(out=fresh[:], in0=i_gate[:], in1=g_gate[:])
         nc.vector.tensor_add(out=c_next[:], in0=c_next[:], in1=fresh[:])
         nc.scalar.activation(out=tanh_c[:], in_=c_next[:], func=ACT.Tanh)
 
         bias = broadcast_bias(3)
-        acc = gate_sums(3)
+        halves = (range(0, BLOCKS // 2), range(BLOCKS // 2, BLOCKS))
+        acc_of_half = [gate_sums(3, blocks) for blocks in halves]
         nc.sync.dma_start(out=out_1, in_=c_next[:])
-        activate(acc, bias, ACT.Sigmoid, o_gate)
-        for j in range(BLOCKS):
-            cols = slice(N_TILE * j, N_TILE * (j + 1))
-            nc.vector.tensor_mul(out=h_next[:, cols], in0=o_gate[:, cols], in1=tanh_c[:, cols])
-            nc.sync.dma_start(out=out_0[:, cols], in_=h_next[:, cols])
+        for acc, blocks in zip(acc_of_half, halves):
+            activate(acc, blocks, bias, ACT.Sigmoid, o_gate)
+            for j in blocks:
+                cols = block_columns(j)
+                nc.vector.tensor_mul(out=h_next[:, cols], in0=o_gate[:, cols], in1=tanh_c[:, cols])
+                nc.sync.dma_start(out=out_0[:, cols], in_=h_next[:, cols])

@@ -82,22 +82,29 @@ def tile_my_lstm_cell_w_kernel(
         bias_rows = keep.tile([P, N_TILE], BF16)
         nc.vector.memset(bias_rows[:], 0.0)
 
-        planes = [keep.tile([P, 2, HID], U8, name="planes%d" % g, align_bytes=64) for g in range(GATES)]
-        for g in range(GATES):
-            nc.vector.memset(planes[g][:].bitcast(I32), 0)
+        r_planes = [keep.tile([P, HID], U8, name="r_planes%d" % g, align_bytes=64) for g in range(GATES)]
+        w_planes = [keep.tile([P, HID], U8, name="w_planes%d" % g, align_bytes=64) for g in range(GATES // 2)]
+        for tile in (r_planes[0], w_planes[0], r_planes[1], r_planes[2], w_planes[1], r_planes[3]):
+            nc.vector.memset(tile[:].bitcast(I32), 0)
 
         for g, (w_words, w_scales, b, r_words, r_scales) in enumerate(gate_inputs):
             nc.gpsimd.dma_start(
                 out=bias_rows[BLOCKS * g : BLOCKS * (g + 1), :], in_=b.rearrange("(j n) -> j n", n=N_TILE)
             )
-        for g, (w_words, w_scales, b, r_words, r_scales) in enumerate(gate_inputs):
-            for operand, scales in enumerate((w_scales, r_scales)):
-                rows = 4 * scales.shape[0]
-                for q in range(QUADRANTS):
-                    nc.gpsimd.dma_start(
-                        out=planes[g][32 * q : 32 * q + rows, operand, :].bitcast(F32),
-                        in_=scales[:, 4 * q : 4 * q + 4, :].bitcast(F32),
-                    )
+        def load_scales(tile, first, scales):
+            rows = 4 * scales.shape[0]
+            for q in range(QUADRANTS):
+                nc.gpsimd.dma_start(
+                    out=tile[32 * q + first : 32 * q + first + rows, :].bitcast(F32),
+                    in_=scales[:, 4 * q : 4 * q + 4, :].bitcast(F32),
+                )
+
+        for pair in range(GATES // 2):
+            even, odd = gate_inputs[2 * pair], gate_inputs[2 * pair + 1]
+            load_scales(r_planes[2 * pair], 0, even[4])
+            load_scales(w_planes[pair], 0, even[1])
+            load_scales(w_planes[pair], 8, odd[1])
+            load_scales(r_planes[2 * pair + 1], 0, odd[4])
 
         xh = keep.tile([P, IN_LEN + HID], BF16)
         c_prev_sb = keep.tile([P, HID], BF16)
@@ -150,9 +157,11 @@ def tile_my_lstm_cell_w_kernel(
             w_words, w_scales, b, r_words, r_scales = gate_inputs[g]
             loaded = slice(N_TILE * blocks[0], N_TILE * (blocks[-1] + 1))
             acc = [psum_acc.tile([P, N_TILE], F32, name="acc%d" % j, tag="acc") for j in blocks]
-            for c in range(PASSES):
+            order = [c for c in range(X_PASSES, PASSES)] + [c for c in range(X_PASSES)]
+            for c in order:
                 operand = 0 if c < X_PASSES else 1
                 group = c if c < X_PASSES else c - X_PASSES
+                plane = r_planes[g][4 * group : P, :] if operand else w_planes[g // 2][8 * (g % 2) + 4 * group : P, :]
                 words = stream.tile([P, N_TILE * len(blocks)], U32, tag="words", align_bytes=64)
                 nc.sync.dma_start(
                     out=words[:].bitcast(I32),
@@ -164,9 +173,9 @@ def tile_my_lstm_cell_w_kernel(
                         lhsT=act_codes[:, P * c : P * (c + 1)].bitcast(FP8X4),
                         lhsT_scale=act_scales[:, P * c : P * (c + 1)],
                         rhs=words[:, block_columns(place)].bitcast(FP8X4),
-                        rhs_scale=planes[g][4 * group : P, operand, block_columns(j)],
-                        start=(c == 0),
-                        stop=(c == PASSES - 1),
+                        rhs_scale=plane[:, block_columns(j)],
+                        start=(c == order[0]),
+                        stop=(c == order[-1]),
                     )
             return acc
 

@@ -69,7 +69,7 @@ def tile_my_lstm_cell_w_kernel(
         tc.manual_schedule(),
         tc.tile_pool(name="keep", bufs=1) as keep,
         tc.tile_pool(name="stream", bufs=WORD_BUFS) as stream,
-        tc.tile_pool(name="bias", bufs=2) as bias_pool,
+        tc.tile_pool(name="bias", bufs=GATES) as bias_pool,
         tc.tile_pool(name="sums", bufs=BLOCKS) as sums_pool,
         tc.psum_pool(name="acc", bufs=6) as psum_acc,
         tc.psum_pool(name="setup", bufs=2) as psum_setup,
@@ -153,12 +153,13 @@ def tile_my_lstm_cell_w_kernel(
         def block_columns(j):
             return slice(N_TILE * j, N_TILE * (j + 1))
 
-        def gate_sums(g, blocks):
+        order = [c for c in range(X_PASSES, PASSES)] + [c for c in range(X_PASSES)]
+
+        def gate_sums(g, loads):
             w_words, w_scales, b, r_words, r_scales = gate_inputs[g]
-            loaded = slice(N_TILE * blocks[0], N_TILE * (blocks[-1] + 1))
-            acc = [psum_acc.tile([P, N_TILE], F32, name="acc%d" % j, tag="acc") for j in blocks]
-            order = [c for c in range(X_PASSES, PASSES)] + [c for c in range(X_PASSES)]
-            for c in order:
+            acc = [psum_acc.tile([P, N_TILE], F32, name="acc%d" % j, tag="acc") for j in range(BLOCKS)]
+            for c, blocks in loads:
+                loaded = slice(N_TILE * blocks[0], N_TILE * (blocks[-1] + 1))
                 operand = 0 if c < X_PASSES else 1
                 group = c if c < X_PASSES else c - X_PASSES
                 plane = r_planes[g][4 * group : P, :] if operand else w_planes[g // 2][8 * (g % 2) + 4 * group : P, :]
@@ -169,7 +170,7 @@ def tile_my_lstm_cell_w_kernel(
                 )
                 for place, j in enumerate(blocks):
                     nc.tensor.matmul_mx(
-                        out=acc[place][:],
+                        out=acc[j][:],
                         lhsT=act_codes[:, P * c : P * (c + 1)].bitcast(FP8X4),
                         lhsT_scale=act_scales[:, P * c : P * (c + 1)],
                         rhs=words[:, block_columns(place)].bitcast(FP8X4),
@@ -179,11 +180,15 @@ def tile_my_lstm_cell_w_kernel(
                     )
             return acc
 
-        def activate(acc, blocks, bias, func, gate):
-            for place, j in enumerate(blocks):
+        def activate(acc, blocks, bias, func, gate, parts=1):
+            width = N_TILE // parts
+            for j in blocks:
                 sums = sums_pool.tile([P, N_TILE], F32)
-                nc.vector.tensor_tensor(out=sums[:], in0=acc[place][:], in1=bias[:, block_columns(j)], op=ADD)
-                nc.scalar.activation(out=gate[:, block_columns(j)], in_=sums[:], func=func)
+                for part in range(parts):
+                    inner = slice(width * part, width * (part + 1))
+                    cols = slice(N_TILE * j + width * part, N_TILE * j + width * (part + 1))
+                    nc.vector.tensor_tensor(out=sums[:, inner], in0=acc[j][:, inner], in1=bias[:, cols], op=ADD)
+                    nc.scalar.activation(out=gate[:, cols], in_=sums[:, inner], func=func)
 
         f_gate = keep.tile([P, HID], F32)
         i_gate = keep.tile([P, HID], F32)
@@ -195,26 +200,27 @@ def tile_my_lstm_cell_w_kernel(
         h_next = keep.tile([P, HID], F32)
 
         all_blocks = range(BLOCKS)
-        bias = broadcast_bias(0)
-        activate(gate_sums(0, all_blocks), all_blocks, bias, ACT.Sigmoid, f_gate)
+        biases = [broadcast_bias(g) for g in range(GATES)]
+        whole = [(c, all_blocks) for c in order]
+        activate(gate_sums(0, whole), all_blocks, biases[0], ACT.Sigmoid, f_gate)
         nc.vector.tensor_mul(out=c_next[:], in0=f_gate[:], in1=c_prev_sb[:])
 
-        bias = broadcast_bias(1)
-        activate(gate_sums(1, all_blocks), all_blocks, bias, ACT.Sigmoid, i_gate)
+        activate(gate_sums(1, whole), all_blocks, biases[1], ACT.Sigmoid, i_gate)
 
-        bias = broadcast_bias(2)
-        activate(gate_sums(2, all_blocks), all_blocks, bias, ACT.Tanh, g_gate)
+        activate(gate_sums(2, whole), all_blocks, biases[2], ACT.Tanh, g_gate)
         nc.vector.tensor_mul(out=fresh[:], in0=i_gate[:], in1=g_gate[:])
         nc.vector.tensor_add(out=c_next[:], in0=c_next[:], in1=fresh[:])
         nc.scalar.activation(out=tanh_c[:], in_=c_next[:], func=ACT.Tanh)
 
-        bias = broadcast_bias(3)
-        halves = (range(0, BLOCKS // 2), range(BLOCKS // 2, BLOCKS))
-        acc_of_half = [gate_sums(3, blocks) for blocks in halves]
+        head, rest = order[: PASSES // 2], order[PASSES // 2 :]
+        groups = (range(0, 2), range(2, 3), range(3, 4))
+        acc = gate_sums(3, [(c, all_blocks) for c in head] + [(c, blocks) for blocks in groups for c in rest])
         nc.sync.dma_start(out=out_1, in_=c_next[:])
-        for acc, blocks in zip(acc_of_half, halves):
-            activate(acc, blocks, bias, ACT.Sigmoid, o_gate)
-            for j in blocks:
-                cols = block_columns(j)
+        for j in all_blocks:
+            parts = 2 if j == BLOCKS - 1 else 1
+            width = N_TILE // parts
+            activate(acc, range(j, j + 1), biases[3], ACT.Sigmoid, o_gate, parts)
+            for part in range(parts):
+                cols = slice(N_TILE * j + width * part, N_TILE * j + width * (part + 1))
                 nc.vector.tensor_mul(out=h_next[:, cols], in0=o_gate[:, cols], in1=tanh_c[:, cols])
-                nc.sync.dma_start(out=out_0[:, cols], in_=h_next[:, cols])
+            nc.sync.dma_start(out=out_0[:, block_columns(j)], in_=h_next[:, block_columns(j)])

@@ -212,15 +212,16 @@ def tile_my_lstm_cell_w_kernel(
         nc.vector.tensor_add(out=c_next[:], in0=c_next[:], in1=fresh[:])
         nc.scalar.activation(out=tanh_c[:], in_=c_next[:], func=ACT.Tanh)
 
-        head, rest = order[: PASSES // 2], order[PASSES // 2 :]
+        head, rest = order[:2], order[2:]
         groups = (range(0, 2), range(2, 3), range(3, 4))
         acc = gate_sums(3, [(c, all_blocks) for c in head] + [(c, blocks) for blocks in groups for c in rest])
         nc.sync.dma_start(out=out_1, in_=c_next[:])
-        for j in all_blocks:
-            parts = 2 if j == BLOCKS - 1 else 1
+        for blocks in groups:
+            parts = 2 if blocks[-1] == BLOCKS - 1 else 1
             width = N_TILE // parts
-            activate(acc, range(j, j + 1), biases[3], ACT.Sigmoid, o_gate, parts)
-            for part in range(parts):
-                cols = slice(N_TILE * j + width * part, N_TILE * j + width * (part + 1))
-                nc.vector.tensor_mul(out=h_next[:, cols], in0=o_gate[:, cols], in1=tanh_c[:, cols])
-            nc.sync.dma_start(out=out_0[:, block_columns(j)], in_=h_next[:, block_columns(j)])
+            activate(acc, blocks, biases[3], ACT.Sigmoid, o_gate, parts)
+            for j in blocks:
+                for part in range(parts):
+                    cols = slice(N_TILE * j + width * part, N_TILE * j + width * (part + 1))
+                    nc.vector.tensor_mul(out=h_next[:, cols], in0=o_gate[:, cols], in1=tanh_c[:, cols])
+                nc.sync.dma_start(out=out_0[:, block_columns(j)], in_=h_next[:, block_columns(j)])

@@ -91,20 +91,20 @@ def tile_my_lstm_cell_w_kernel(
             nc.gpsimd.dma_start(
                 out=bias_rows[BLOCKS * g : BLOCKS * (g + 1), :], in_=b.rearrange("(j n) -> j n", n=N_TILE)
             )
-        def load_scales(tile, first, scales):
-            rows = 4 * scales.shape[0]
+        def load_scales(*parts):
             for q in range(QUADRANTS):
-                nc.gpsimd.dma_start(
-                    out=tile[32 * q + first : 32 * q + first + rows, :].bitcast(F32),
-                    in_=scales[:, 4 * q : 4 * q + 4, :].bitcast(F32),
-                )
+                for tile, first, scales in parts:
+                    rows = 4 * scales.shape[0]
+                    nc.gpsimd.dma_start(
+                        out=tile[32 * q + first : 32 * q + first + rows, :].bitcast(F32),
+                        in_=scales[:, 4 * q : 4 * q + 4, :].bitcast(F32),
+                    )
 
         for pair in range(GATES // 2):
             even, odd = gate_inputs[2 * pair], gate_inputs[2 * pair + 1]
-            load_scales(r_planes[2 * pair], 0, even[4])
-            load_scales(w_planes[pair], 0, even[1])
-            load_scales(w_planes[pair], 8, odd[1])
-            load_scales(r_planes[2 * pair + 1], 0, odd[4])
+            load_scales((r_planes[2 * pair], 0, even[4]))
+            load_scales((w_planes[pair], 0, even[1]), (w_planes[pair], 8, odd[1]))
+            load_scales((r_planes[2 * pair + 1], 0, odd[4]))
 
         xh = keep.tile([P, IN_LEN + HID], BF16)
         c_prev_sb = keep.tile([P, HID], BF16)

@@ -82,27 +82,39 @@ def tile_my_lstm_cell_w_kernel(
         bias_rows = keep.tile([P, N_TILE], BF16)
         nc.vector.memset(bias_rows[:], 0.0)
 
+        c_packed = keep.tile([P, 2, HID], BF16)
+
         r_planes = [keep.tile([P, HID], U8, name="r_planes%d" % g, align_bytes=64) for g in range(GATES)]
         w_planes = [keep.tile([P, HID], U8, name="w_planes%d" % g, align_bytes=64) for g in range(GATES // 2)]
-        for tile in (r_planes[0], w_planes[0], r_planes[1], r_planes[2], w_planes[1], r_planes[3]):
+        nc.vector.memset(r_planes[0][:].bitcast(I32), 0)
+        nc.vector.memset(c_packed[:].rearrange("p r n -> p (r n)").bitcast(I32), 0)
+        for tile in (w_planes[0], r_planes[1], r_planes[2], w_planes[1], r_planes[3]):
             nc.vector.memset(tile[:].bitcast(I32), 0)
 
         for g, (w_words, w_scales, b, r_words, r_scales) in enumerate(gate_inputs):
-            nc.gpsimd.dma_start(
+            nc.scalar.dma_start(
                 out=bias_rows[BLOCKS * g : BLOCKS * (g + 1), :], in_=b.rearrange("(j n) -> j n", n=N_TILE)
             )
-        def load_scales(*parts):
-            for q in range(QUADRANTS):
+        def load_scales(*parts, quadrants=range(QUADRANTS), fill=False):
+            for q in quadrants:
                 for tile, first, scales in parts:
                     rows = 4 * scales.shape[0]
                     nc.gpsimd.dma_start(
                         out=tile[32 * q + first : 32 * q + first + rows, :].bitcast(F32),
                         in_=scales[:, 4 * q : 4 * q + 4, :].bitcast(F32),
                     )
+                if fill:
+                    nc.gpsimd.dma_start(
+                        out=c_packed[32 * q + 16 : 32 * q + 32, :, :],
+                        in_=c_prev[32 * q : 32 * q + 32, :].rearrange("(b a r) n -> a b (r n)", b=4, r=2),
+                    )
 
         for pair in range(GATES // 2):
             even, odd = gate_inputs[2 * pair], gate_inputs[2 * pair + 1]
-            load_scales((r_planes[2 * pair], 0, even[4]))
+            if pair == 0:
+                load_scales((r_planes[0], 0, even[4]), quadrants=(0, 2, 1, 3), fill=True)
+            else:
+                load_scales((r_planes[2 * pair], 0, even[4]))
             load_scales((w_planes[pair], 0, even[1]), (w_planes[pair], 8, odd[1]))
             load_scales((r_planes[2 * pair + 1], 0, odd[4]))
 
@@ -110,7 +122,16 @@ def tile_my_lstm_cell_w_kernel(
         c_prev_sb = keep.tile([P, HID], BF16)
         nc.sync.dma_start(out=xh[:, :IN_LEN], in_=x)
         nc.sync.dma_start(out=xh[:, IN_LEN:], in_=h)
-        nc.sync.dma_start(out=c_prev_sb[:], in_=c_prev)
+
+        row_of = keep.tile([P, 2, P], BF16)
+        nc.vector.memset(row_of[:], 0.0)
+        for r in range(2):
+            nc.vector.tensor_copy(
+                out=row_of[:, r, :].rearrange("p (q b a s) -> p q b a s", q=QUADRANTS, b=4, s=2)[:, :, :, :, r],
+                in_=ident_bf16[:].rearrange("p (q j) -> p q j", q=QUADRANTS)[:, :, 16:32].rearrange(
+                    "p q (a b) -> p q b a", b=4
+                ),
+            )
 
         xh_words = xh[:].bitcast(F32)
         grouped = keep.tile([P, PASSES * P * PACK], BF16, align_bytes=64)
@@ -202,7 +223,19 @@ def tile_my_lstm_cell_w_kernel(
         all_blocks = range(BLOCKS)
         biases = [broadcast_bias(g) for g in range(GATES)]
         whole = [(c, all_blocks) for c in order]
-        activate(gate_sums(0, whole), all_blocks, biases[0], ACT.Sigmoid, f_gate)
+        acc = gate_sums(0, whole)
+        for j in all_blocks:
+            unpacked = psum_setup.tile([P, N_TILE], F32, tag="setup")
+            for r in range(2):
+                nc.tensor.matmul(
+                    out=unpacked[:],
+                    lhsT=row_of[:, r, :],
+                    rhs=c_packed[:, r, block_columns(j)],
+                    start=(r == 0),
+                    stop=(r == 1),
+                )
+            nc.scalar.copy(out=c_prev_sb[:, block_columns(j)], in_=unpacked[:])
+        activate(acc, all_blocks, biases[0], ACT.Sigmoid, f_gate)
         nc.vector.tensor_mul(out=c_next[:], in0=f_gate[:], in1=c_prev_sb[:])
 
         activate(gate_sums(1, whole), all_blocks, biases[1], ACT.Sigmoid, i_gate)

@@ -24,7 +24,7 @@ BLOCKS = HID // N_TILE
 QUADRANTS = 4
 WORDS_PER_PASS = K_PASS // 2
 
-WORD_BUFS = 12
+WORD_BUFS = 15
 
 FLOPS = 2 * P * (IN_LEN + HID) * GATES * HID
 
@@ -95,7 +95,7 @@ def tile_my_lstm_cell_w_kernel(
             nc.scalar.dma_start(
                 out=bias_rows[BLOCKS * g : BLOCKS * (g + 1), :], in_=b.rearrange("(j n) -> j n", n=N_TILE)
             )
-        def load_scales(*parts, quadrants=range(QUADRANTS), fill=False):
+        def load_scales(*parts, quadrants=range(QUADRANTS), fill=None):
             for q in quadrants:
                 for tile, first, scales in parts:
                     rows = 4 * scales.shape[0]
@@ -103,20 +103,18 @@ def tile_my_lstm_cell_w_kernel(
                         out=tile[32 * q + first : 32 * q + first + rows, :].bitcast(F32),
                         in_=scales[:, 4 * q : 4 * q + 4, :].bitcast(F32),
                     )
-                if fill:
+                if fill is not None:
                     nc.gpsimd.dma_start(
-                        out=c_packed[32 * q + 16 : 32 * q + 32, :, :],
-                        in_=c_prev[32 * q : 32 * q + 32, :].rearrange("(b a r) n -> a b (r n)", b=4, r=2),
+                        out=c_packed[32 * q + 16 : 32 * q + 32, fill, :],
+                        in_=c_prev[32 * q : 32 * q + 32, :].rearrange("(b a r) n -> a b r n", b=4, r=2)[:, :, fill, :],
                     )
 
         for pair in range(GATES // 2):
             even, odd = gate_inputs[2 * pair], gate_inputs[2 * pair + 1]
-            if pair == 0:
-                load_scales((r_planes[0], 0, even[4]), quadrants=(0, 2, 1, 3), fill=True)
-            else:
-                load_scales((r_planes[2 * pair], 0, even[4]))
+            quadrants, fills = ((0, 2, 1, 3), (0, 1)) if pair == 0 else (range(QUADRANTS), (None, None))
+            load_scales((r_planes[2 * pair], 0, even[4]), quadrants=quadrants, fill=fills[0])
             load_scales((w_planes[pair], 0, even[1]), (w_planes[pair], 8, odd[1]))
-            load_scales((r_planes[2 * pair + 1], 0, odd[4]))
+            load_scales((r_planes[2 * pair + 1], 0, odd[4]), quadrants=quadrants, fill=fills[1])
 
         xh = keep.tile([P, IN_LEN + HID], BF16)
         c_prev_sb = keep.tile([P, HID], BF16)
@@ -214,16 +212,18 @@ def tile_my_lstm_cell_w_kernel(
         f_gate = keep.tile([P, HID], F32)
         i_gate = keep.tile([P, HID], F32)
         g_gate = keep.tile([P, HID], F32)
-        o_gate = keep.tile([P, HID], F32)
-        fresh = keep.tile([P, HID], F32)
+        o_gate = f_gate
+        fresh = i_gate
         c_next = keep.tile([P, HID], F32)
         tanh_c = keep.tile([P, HID], F32)
-        h_next = keep.tile([P, HID], F32)
+        h_next = g_gate
 
         all_blocks = range(BLOCKS)
         biases = [broadcast_bias(g) for g in range(GATES)]
         whole = [(c, all_blocks) for c in order]
-        acc = gate_sums(0, whole)
+        activate(gate_sums(0, whole), all_blocks, biases[0], ACT.Sigmoid, f_gate)
+
+        acc = gate_sums(1, whole)
         for j in all_blocks:
             unpacked = psum_setup.tile([P, N_TILE], F32, tag="setup")
             for r in range(2):
@@ -235,10 +235,8 @@ def tile_my_lstm_cell_w_kernel(
                     stop=(r == 1),
                 )
             nc.scalar.copy(out=c_prev_sb[:, block_columns(j)], in_=unpacked[:])
-        activate(acc, all_blocks, biases[0], ACT.Sigmoid, f_gate)
+        activate(acc, all_blocks, biases[1], ACT.Sigmoid, i_gate)
         nc.vector.tensor_mul(out=c_next[:], in0=f_gate[:], in1=c_prev_sb[:])
-
-        activate(gate_sums(1, whole), all_blocks, biases[1], ACT.Sigmoid, i_gate)
 
         activate(gate_sums(2, whole), all_blocks, biases[2], ACT.Tanh, g_gate)
         nc.vector.tensor_mul(out=fresh[:], in0=i_gate[:], in1=g_gate[:])

@@ -82,13 +82,19 @@ def tile_my_lstm_cell_w_kernel(
         bias_rows = keep.tile([P, N_TILE], BF16)
         nc.vector.memset(bias_rows[:], 0.0)
 
+        x_packed = keep.tile([P, 2, IN_LEN], BF16)
         c_packed = keep.tile([P, 2, HID], BF16)
 
         r_planes = [keep.tile([P, HID], U8, name="r_planes%d" % g, align_bytes=64) for g in range(GATES)]
         w_planes = [keep.tile([P, HID], U8, name="w_planes%d" % g, align_bytes=64) for g in range(GATES // 2)]
+        flat_x = x_packed[:].rearrange("p r n -> p (r n)")
+        flat_c = c_packed[:].rearrange("p r n -> p (r n)")
         nc.vector.memset(r_planes[0][:].bitcast(I32), 0)
-        nc.vector.memset(c_packed[:].rearrange("p r n -> p (r n)").bitcast(I32), 0)
-        for tile in (w_planes[0], r_planes[1], r_planes[2], w_planes[1], r_planes[3]):
+        nc.vector.memset(flat_x.bitcast(I32), 0)
+        nc.vector.memset(w_planes[0][:].bitcast(I32), 0)
+        nc.vector.memset(r_planes[1][:].bitcast(I32), 0)
+        nc.vector.memset(flat_c.bitcast(I32), 0)
+        for tile in (r_planes[2], w_planes[1], r_planes[3]):
             nc.vector.memset(tile[:].bitcast(I32), 0)
 
         for g, (w_words, w_scales, b, r_words, r_scales) in enumerate(gate_inputs):
@@ -104,22 +110,22 @@ def tile_my_lstm_cell_w_kernel(
                         in_=scales[:, 4 * q : 4 * q + 4, :].bitcast(F32),
                     )
                 if fill is not None:
+                    packed, source = fill
                     nc.gpsimd.dma_start(
-                        out=c_packed[32 * q + 16 : 32 * q + 32, fill, :],
-                        in_=c_prev[32 * q : 32 * q + 32, :].rearrange("(b a r) n -> a b r n", b=4, r=2)[:, :, fill, :],
+                        out=packed[32 * q + 16 : 32 * q + 32, :],
+                        in_=source[32 * q : 32 * q + 32, :].rearrange("(b a r) n -> a b (r n)", b=4, r=2),
                     )
 
         for pair in range(GATES // 2):
             even, odd = gate_inputs[2 * pair], gate_inputs[2 * pair + 1]
-            quadrants, fills = ((0, 2, 1, 3), (0, 1)) if pair == 0 else (range(QUADRANTS), (None, None))
+            quadrants, fills = ((0, 2, 1, 3), ((flat_x, x), (flat_c, c_prev))) if pair == 0 else (range(QUADRANTS), (None, None))
             load_scales((r_planes[2 * pair], 0, even[4]), quadrants=quadrants, fill=fills[0])
             load_scales((w_planes[pair], 0, even[1]), (w_planes[pair], 8, odd[1]))
             load_scales((r_planes[2 * pair + 1], 0, odd[4]), quadrants=quadrants, fill=fills[1])
 
-        xh = keep.tile([P, IN_LEN + HID], BF16)
+        h_sb = keep.tile([P, HID], BF16)
         c_prev_sb = keep.tile([P, HID], BF16)
-        nc.sync.dma_start(out=xh[:, :IN_LEN], in_=x)
-        nc.sync.dma_start(out=xh[:, IN_LEN:], in_=h)
+        nc.sync.dma_start(out=h_sb[:], in_=h)
 
         row_of = keep.tile([P, 2, P], BF16)
         nc.vector.memset(row_of[:], 0.0)
@@ -131,17 +137,17 @@ def tile_my_lstm_cell_w_kernel(
                 ),
             )
 
-        xh_words = xh[:].bitcast(F32)
+        h_words = h_sb[:].bitcast(F32)
         grouped = keep.tile([P, PASSES * P * PACK], BF16, align_bytes=64)
         act_codes = keep.tile([P, PASSES * P], U32, align_bytes=64)
         act_scales = keep.tile([P, PASSES * P], U8, align_bytes=64)
-        for pair in range(PASSES // 2):
+        for pair in range(X_PASSES // 2, PASSES // 2):
             turned = psum_setup.tile([P, 2, 2, P], F32, tag="setup")
             for s in range(2):
-                first = WORDS_PER_PASS * (2 * pair + s)
+                first = WORDS_PER_PASS * (2 * pair + s - X_PASSES)
                 for u in range(2):
                     nc.tensor.transpose(
-                        turned[:, s, u, :], xh_words[:, first + u : first + WORDS_PER_PASS : 2], ident_f32[:]
+                        turned[:, s, u, :], h_words[:, first + u : first + WORDS_PER_PASS : 2], ident_f32[:]
                     )
             values = slice(2 * P * PACK * pair, 2 * P * PACK * (pair + 1))
             columns = slice(2 * P * pair, 2 * P * (pair + 1))
@@ -152,6 +158,28 @@ def tile_my_lstm_cell_w_kernel(
             nc.vector.quantize_mx(
                 out=act_codes[:, columns].bitcast(FP8X4), scales=act_scales[:, columns], in_=grouped[:, values]
             )
+
+        for c in range(X_PASSES):
+            turned = psum_setup.tile([P, PACK, P], F32, tag="setup")
+            for t in range(PACK):
+                for r in range(2):
+                    nc.tensor.matmul(
+                        out=turned[:, t, :],
+                        lhsT=x_packed[:, r, K_PASS * c + t : K_PASS * (c + 1) : PACK],
+                        rhs=row_of[:, r, :],
+                        start=(r == 0),
+                        stop=(r == 1),
+                    )
+            nc.vector.tensor_copy(
+                out=grouped[:, K_PASS * c : K_PASS * (c + 1)].rearrange("p (m t) -> p m t", t=PACK),
+                in_=turned[:].rearrange("p t m -> p m t"),
+            )
+        x_columns = slice(0, P * X_PASSES)
+        nc.vector.quantize_mx(
+            out=act_codes[:, x_columns].bitcast(FP8X4),
+            scales=act_scales[:, x_columns],
+            in_=grouped[:, : K_PASS * X_PASSES],
+        )
 
         def broadcast_bias(g):
             bias = bias_pool.tile([P, HID], BF16)

import concourse.mybir as mybir
from concourse.masks import make_identity

F32 = mybir.dt.float32
BF16 = mybir.dt.bfloat16
I32 = mybir.dt.int32
U32 = mybir.dt.uint32
U8 = mybir.dt.uint8
FP8X4 = mybir.dt.float8_e4m3fn_x4
ACT = mybir.ActivationFunctionType
ADD = mybir.AluOpType.add

P = 128
PACK = 4
K_PASS = P * PACK
IN_LEN = 1024
HID = 2048
X_PASSES = IN_LEN // K_PASS
H_PASSES = HID // K_PASS
PASSES = X_PASSES + H_PASSES
GATES = 4
N_TILE = 512
BLOCKS = HID // N_TILE
QUADRANTS = 4
WORDS_PER_PASS = K_PASS // 2

WORD_BUFS = 15

FLOPS = 2 * P * (IN_LEN + HID) * GATES * HID


def tile_my_lstm_cell_w_kernel(
    tc,
    x,
    h,
    c_prev,
    w1_words,
    w1_scales,
    b1,
    r1_words,
    r1_scales,
    w2_words,
    w2_scales,
    b2,
    r2_words,
    r2_scales,
    w3_words,
    w3_scales,
    b3,
    r3_words,
    r3_scales,
    w4_words,
    w4_scales,
    b4,
    r4_words,
    r4_scales,
    out_0,
    out_1,
):
    nc = tc.nc
    gate_inputs = [
        (w1_words, w1_scales, b1, r1_words, r1_scales),
        (w2_words, w2_scales, b2, r2_words, r2_scales),
        (w3_words, w3_scales, b3, r3_words, r3_scales),
        (w4_words, w4_scales, b4, r4_words, r4_scales),
    ]

    with (
        tc.manual_schedule(),
        tc.tile_pool(name="keep", bufs=1) as keep,
        tc.tile_pool(name="stream", bufs=WORD_BUFS) as stream,
        tc.tile_pool(name="bias", bufs=GATES) as bias_pool,
        tc.tile_pool(name="sums", bufs=BLOCKS) as sums_pool,
        tc.psum_pool(name="acc", bufs=6) as psum_acc,
        tc.psum_pool(name="setup", bufs=2) as psum_setup,
    ):
        ident_f32 = keep.tile([P, P], F32)
        make_identity(nc, ident_f32[:])
        ident_bf16 = keep.tile([P, P], BF16)
        make_identity(nc, ident_bf16[:])

        bias_rows = keep.tile([P, N_TILE], BF16)
        nc.vector.memset(bias_rows[:], 0.0)

        x_packed = keep.tile([P, 2, IN_LEN], BF16)
        c_packed = keep.tile([P, 2, HID], BF16)

        r_planes = [keep.tile([P, HID], U8, name="r_planes%d" % g, align_bytes=64) for g in range(GATES)]
        w_planes = [keep.tile([P, HID], U8, name="w_planes%d" % g, align_bytes=64) for g in range(GATES // 2)]
        flat_x = x_packed[:].rearrange("p r n -> p (r n)")
        flat_c = c_packed[:].rearrange("p r n -> p (r n)")
        nc.vector.memset(r_planes[0][:].bitcast(I32), 0)
        nc.vector.memset(flat_x.bitcast(I32), 0)
        nc.vector.memset(w_planes[0][:].bitcast(I32), 0)
        nc.vector.memset(r_planes[1][:].bitcast(I32), 0)
        nc.vector.memset(flat_c.bitcast(I32), 0)
        for tile in (r_planes[2], w_planes[1], r_planes[3]):
            nc.vector.memset(tile[:].bitcast(I32), 0)

        for g, (w_words, w_scales, b, r_words, r_scales) in enumerate(gate_inputs):
            nc.scalar.dma_start(
                out=bias_rows[BLOCKS * g : BLOCKS * (g + 1), :], in_=b.rearrange("(j n) -> j n", n=N_TILE)
            )
        def load_scales(*parts, quadrants=range(QUADRANTS), fill=None):
            for q in quadrants:
                for tile, first, scales in parts:
                    rows = 4 * scales.shape[0]
                    nc.gpsimd.dma_start(
                        out=tile[32 * q + first : 32 * q + first + rows, :].bitcast(F32),
                        in_=scales[:, 4 * q : 4 * q + 4, :].bitcast(F32),
                    )
                if fill is not None:
                    packed, source = fill
                    nc.gpsimd.dma_start(
                        out=packed[32 * q + 16 : 32 * q + 32, :],
                        in_=source[32 * q : 32 * q + 32, :].rearrange("(b a r) n -> a b (r n)", b=4, r=2),
                    )

        for pair in range(GATES // 2):
            even, odd = gate_inputs[2 * pair], gate_inputs[2 * pair + 1]
            quadrants, fills = ((0, 2, 1, 3), ((flat_x, x), (flat_c, c_prev))) if pair == 0 else (range(QUADRANTS), (None, None))
            load_scales((r_planes[2 * pair], 0, even[4]), quadrants=quadrants, fill=fills[0])
            load_scales((w_planes[pair], 0, even[1]), (w_planes[pair], 8, odd[1]))
            load_scales((r_planes[2 * pair + 1], 0, odd[4]), quadrants=quadrants, fill=fills[1])

        h_sb = keep.tile([P, HID], BF16)
        c_prev_sb = keep.tile([P, HID], BF16)
        nc.sync.dma_start(out=h_sb[:], in_=h)

        row_of = keep.tile([P, 2, P], BF16)
        nc.vector.memset(row_of[:], 0.0)
        for r in range(2):
            nc.vector.tensor_copy(
                out=row_of[:, r, :].rearrange("p (q b a s) -> p q b a s", q=QUADRANTS, b=4, s=2)[:, :, :, :, r],
                in_=ident_bf16[:].rearrange("p (q j) -> p q j", q=QUADRANTS)[:, :, 16:32].rearrange(
                    "p q (a b) -> p q b a", b=4
                ),
            )

        h_words = h_sb[:].bitcast(F32)
        grouped = keep.tile([P, PASSES * P * PACK], BF16, align_bytes=64)
        act_codes = keep.tile([P, PASSES * P], U32, align_bytes=64)
        act_scales = keep.tile([P, PASSES * P], U8, align_bytes=64)
        for pair in range(X_PASSES // 2, PASSES // 2):
            turned = psum_setup.tile([P, 2, 2, P], F32, tag="setup")
            for s in range(2):
                first = WORDS_PER_PASS * (2 * pair + s - X_PASSES)
                for u in range(2):
                    nc.tensor.transpose(
                        turned[:, s, u, :], h_words[:, first + u : first + WORDS_PER_PASS : 2], ident_f32[:]
                    )
            values = slice(2 * P * PACK * pair, 2 * P * PACK * (pair + 1))
            columns = slice(2 * P * pair, 2 * P * (pair + 1))
            nc.vector.tensor_copy(
                out=grouped[:, values].bitcast(F32).rearrange("p (s m u) -> p s m u", s=2, u=2),
                in_=turned[:].rearrange("p s u m -> p s m u"),
            )
            nc.vector.quantize_mx(
                out=act_codes[:, columns].bitcast(FP8X4), scales=act_scales[:, columns], in_=grouped[:, values]
            )

        for c in range(X_PASSES):
            turned = psum_setup.tile([P, PACK, P], F32, tag="setup")
            for t in range(PACK):
                for r in range(2):
                    nc.tensor.matmul(
                        out=turned[:, t, :],
                        lhsT=x_packed[:, r, K_PASS * c + t : K_PASS * (c + 1) : PACK],
                        rhs=row_of[:, r, :],
                        start=(r == 0),
                        stop=(r == 1),
                    )
            nc.vector.tensor_copy(
                out=grouped[:, K_PASS * c : K_PASS * (c + 1)].rearrange("p (m t) -> p m t", t=PACK),
                in_=turned[:].rearrange("p t m -> p m t"),
            )
        x_columns = slice(0, P * X_PASSES)
        nc.vector.quantize_mx(
            out=act_codes[:, x_columns].bitcast(FP8X4),
            scales=act_scales[:, x_columns],
            in_=grouped[:, : K_PASS * X_PASSES],
        )

        def broadcast_bias(g):
            bias = bias_pool.tile([P, HID], BF16)
            for half in range(2):
                spread = psum_setup.tile([P, 2 * N_TILE], BF16, tag="setup")
                for s in range(2):
                    row = BLOCKS * g + 2 * half + s
                    nc.tensor.matmul(
                        out=spread[:, N_TILE * s : N_TILE * (s + 1)],
                        lhsT=ident_bf16[:, row : row + 1].to_broadcast([P, P]),
                        rhs=bias_rows[:],
                        start=True,
                        stop=True,
                    )
                nc.scalar.copy(out=bias[:, 2 * N_TILE * half : 2 * N_TILE * (half + 1)], in_=spread[:])
            return bias

        def block_columns(j):
            return slice(N_TILE * j, N_TILE * (j + 1))

        order = [c for c in range(X_PASSES, PASSES)] + [c for c in range(X_PASSES)]

        def gate_sums(g, loads):
            w_words, w_scales, b, r_words, r_scales = gate_inputs[g]
            acc = [psum_acc.tile([P, N_TILE], F32, name="acc%d" % j, tag="acc") for j in range(BLOCKS)]
            for c, blocks in loads:
                loaded = slice(N_TILE * blocks[0], N_TILE * (blocks[-1] + 1))
                operand = 0 if c < X_PASSES else 1
                group = c if c < X_PASSES else c - X_PASSES
                plane = r_planes[g][4 * group : P, :] if operand else w_planes[g // 2][8 * (g % 2) + 4 * group : P, :]
                words = stream.tile([P, N_TILE * len(blocks)], U32, tag="words", align_bytes=64)
                nc.sync.dma_start(
                    out=words[:].bitcast(I32),
                    in_=(w_words, r_words)[operand][group][:, loaded, :].rearrange("p n t -> p (n t)").bitcast(I32),
                )
                for place, j in enumerate(blocks):
                    nc.tensor.matmul_mx(
                        out=acc[j][:],
                        lhsT=act_codes[:, P * c : P * (c + 1)].bitcast(FP8X4),
                        lhsT_scale=act_scales[:, P * c : P * (c + 1)],
                        rhs=words[:, block_columns(place)].bitcast(FP8X4),
                        rhs_scale=plane[:, block_columns(j)],
                        start=(c == order[0]),
                        stop=(c == order[-1]),
                    )
            return acc

        def activate(acc, blocks, bias, func, gate, parts=1):
            width = N_TILE // parts
            for j in blocks:
                sums = sums_pool.tile([P, N_TILE], F32)
                for part in range(parts):
                    inner = slice(width * part, width * (part + 1))
                    cols = slice(N_TILE * j + width * part, N_TILE * j + width * (part + 1))
                    nc.vector.tensor_tensor(out=sums[:, inner], in0=acc[j][:, inner], in1=bias[:, cols], op=ADD)
                    nc.scalar.activation(out=gate[:, cols], in_=sums[:, inner], func=func)

        f_gate = keep.tile([P, HID], F32)
        i_gate = keep.tile([P, HID], F32)
        g_gate = keep.tile([P, HID], F32)
        o_gate = f_gate
        fresh = i_gate
        c_next = keep.tile([P, HID], F32)
        tanh_c = keep.tile([P, HID], F32)
        h_next = g_gate

        all_blocks = range(BLOCKS)
        biases = [broadcast_bias(g) for g in range(GATES)]
        whole = [(c, all_blocks) for c in order]
        activate(gate_sums(0, whole), all_blocks, biases[0], ACT.Sigmoid, f_gate)

        acc = gate_sums(1, whole)
        for j in all_blocks:
            unpacked = psum_setup.tile([P, N_TILE], F32, tag="setup")
            for r in range(2):
                nc.tensor.matmul(
                    out=unpacked[:],
                    lhsT=row_of[:, r, :],
                    rhs=c_packed[:, r, block_columns(j)],
                    start=(r == 0),
                    stop=(r == 1),
                )
            nc.scalar.copy(out=c_prev_sb[:, block_columns(j)], in_=unpacked[:])
        activate(acc, all_blocks, biases[1], ACT.Sigmoid, i_gate)
        nc.vector.tensor_mul(out=c_next[:], in0=f_gate[:], in1=c_prev_sb[:])

        activate(gate_sums(2, whole), all_blocks, biases[2], ACT.Tanh, g_gate)
        nc.vector.tensor_mul(out=fresh[:], in0=i_gate[:], in1=g_gate[:])
        nc.vector.tensor_add(out=c_next[:], in0=c_next[:], in1=fresh[:])
        nc.scalar.activation(out=tanh_c[:], in_=c_next[:], func=ACT.Tanh)

        head, rest = order[:2], order[2:]
        groups = (range(0, 2), range(2, 3), range(3, 4))
        acc = gate_sums(3, [(c, all_blocks) for c in head] + [(c, blocks) for blocks in groups for c in rest])
        nc.sync.dma_start(out=out_1, in_=c_next[:])
        for blocks in groups:
            parts = 2 if blocks[-1] == BLOCKS - 1 else 1
            width = N_TILE // parts
            activate(acc, blocks, biases[3], ACT.Sigmoid, o_gate, parts)
            for j in blocks:
                for part in range(parts):
                    cols = slice(N_TILE * j + width * part, N_TILE * j + width * (part + 1))
                    nc.vector.tensor_mul(out=h_next[:, cols], in0=o_gate[:, cols], in1=tanh_c[:, cols])
                nc.sync.dma_start(out=out_0[:, block_columns(j)], in_=h_next[:, block_columns(j)])
